import numpy as np
import ml_dtypes


def mxq(x, axis, fmt="e4m3"):
    dtype, down = {"e4m3": (ml_dtypes.float8_e4m3fn, 7), "e5m2": (ml_dtypes.float8_e5m2, 14)}[fmt]
    v = np.moveaxis(np.asarray(x, np.float32).astype(ml_dtypes.bfloat16).astype(np.float64), axis, -1)
    blocks = v.reshape(v.shape[:-1] + (-1, 32))
    amax = np.abs(blocks).max(-1, keepdims=True)
    byte = np.maximum(np.where(amax > 0, np.frexp(amax)[1] - 1 + 127, 0) - down, 1)
    scale = np.exp2(byte - 127.0)
    codes = (blocks / scale).astype(np.float32).astype(dtype).astype(np.float64)
    return np.moveaxis((codes * scale).reshape(v.shape), -1, axis)


WIDE = False


def mx_kscale(k):
    if not WIDE:
        return np.ones(k)
    levels = np.array([10, -10, 5, -5, 0])
    a = np.random.permutation(np.resize(levels, k // 512 * 4)).reshape(k // 512, 4)
    idx = np.arange(k)
    return np.exp2(a[idx // 512, idx % 128 // 32])


BF16 = ml_dtypes.bfloat16


def bf(x):
    return np.asarray(x, np.float32).astype(BF16)


def f64(x):
    return np.asarray(x).astype(np.float64)


B, N, E, H, C = 1, 1024, 2048, 8, 512
D = E // H


def decay_gammas():
    return 1.0 - np.exp(np.linspace(np.log(2.0 ** -5), np.log(2.0 ** -9), H))


def setup_inputs():
    t = mx_kscale(N)
    return {"q_rot": bf(np.random.standard_normal((B, H, N, D))),
            "k_scaled": bf(np.random.standard_normal((B, H, N, D)) / np.sqrt(D) * t[:, None]),
            "v": bf(np.random.standard_normal((B, H, N, D)) * 0.5 / t[:, None])}


def reference(q_rot, k_scaled, v):
    q, k = f64(q_rot), f64(k_scaled)
    vq = mxq(f64(v), 2, "e4m3")
    gam = decay_gammas()[:, None, None]
    out = []
    for i in range(N // C):
        lo, hi = i * C, (i + 1) * C
        dist = f64(np.arange(lo, hi))[:, None] - f64(np.arange(hi))[None, :]
        mask = gam ** np.where(dist < 0, np.inf, dist)
        sim = (q[:, :, lo:hi] @ k[:, :, :hi].transpose(0, 1, 3, 2)) * mask[None]
        out.append(mxq(sim, 3, "e4m3") @ vq[:, :, :hi])
    ret = np.concatenate(out, axis=2)
    return ret.transpose(0, 2, 1, 3).reshape(B, N, E)

@@ -1,0 +1,255 @@
+import math
+from contextlib import ExitStack
+
+import concourse.mybir as mybir
+from concourse.masks import make_identity
+
+BF16 = mybir.dt.bfloat16
+F32 = mybir.dt.float32
+U32 = mybir.dt.uint32
+U8 = mybir.dt.uint8
+FP8X4 = mybir.dt.float8_e4m3fn_x4
+
+H = 8
+N = 1024
+D = 256
+P = 128
+PACK = 4
+TILES = N // P
+HALF = TILES // 2
+D_PARTS = D // P
+
+BANKS = [(j, c) for j in range(TILES) for c in range(j // PACK + 1)]
+PAIRS = [(BANKS[b], BANKS[b + 1]) for b in range(0, len(BANKS), 2)]
+MX_LAG = 2
+FAR = 1.0e8
+
+FLOPS = 2 * 2 * H * D * len(BANKS) * P * PACK * P
+
+
+def live_slots(j, c):
+    return min(PACK, j - PACK * c + 1)
+
+
+def log_decay(h):
+    first, last = math.log(2.0 ** -5), math.log(2.0 ** -9)
+    return math.log(1.0 - math.exp(first + (last - first) * h / (H - 1)))
+
+
+def tile_multiscaleretention_pb_kernel(tc, q_rot, k_scaled, v, out):
+    nc = tc.nc
+    out_tiles = out[0].rearrange("(j p) e -> p j e", p=P)
+
+    with ExitStack() as ctx:
+        const = ctx.enter_context(tc.tile_pool(name="const", bufs=1))
+        raw = ctx.enter_context(tc.tile_pool(name="raw", bufs=3))
+        turned = ctx.enter_context(tc.tile_pool(name="turned", bufs=2))
+        decays = ctx.enter_context(tc.tile_pool(name="decays", bufs=3))
+        values_in = ctx.enter_context(tc.tile_pool(name="values_in", bufs=2))
+        packed = ctx.enter_context(tc.tile_pool(name="packed", bufs=4))
+        results = ctx.enter_context(tc.tile_pool(name="results", bufs=3))
+        psum_turn = ctx.enter_context(tc.psum_pool(name="psum_turn", bufs=2))
+        psum_sim = ctx.enter_context(tc.psum_pool(name="psum_sim", bufs=4))
+        psum_ret = ctx.enter_context(tc.psum_pool(name="psum_ret", bufs=2))
+        ctx.enter_context(tc.manual_schedule())
+
+        identity = const.tile([P, P], BF16)
+        make_identity(nc, identity[:])
+
+        distance = const.tile([P, TILES, P], F32)
+        nc.gpsimd.iota(
+            distance[:],
+            pattern=[[-P, TILES], [1, P]],
+            base=P * (TILES - 1),
+            channel_multiplier=-1,
+            allow_small_or_imprecise_dtypes=True,
+        )
+        nc.gpsimd.affine_select(
+            out=distance[:, TILES - 1, :],
+            in_=distance[:, TILES - 1, :],
+            pattern=[[1, P]],
+            compare_op=mybir.AluOpType.is_ge,
+            fill=FAR,
+            base=0,
+            channel_multiplier=-1,
+        )
+
+        grouped = {}
+        for k, pair in enumerate(PAIRS):
+            grouped[k] = const.tile([P, 2, P, PACK], BF16, name="grouped%d" % k, align_bytes=64)
+            for i, (j, c) in enumerate(pair):
+                if live_slots(j, c) < PACK:
+                    nc.vector.memset(grouped[k][:, i], 0.0)
+
+        q_raw, k_raw, v_raw = {}, {}, {}
+        q_turned, k_turned = {}, {}
+        decay = {}
+        v_grouped, v_codes, v_scales = {}, {}, {}
+        sim = {}
+        codes, scales = {}, {}
+        ret = {}
+        result = {}
+
+        def load_half(tile_of, source, h, half):
+            rows = source[0, h, half * HALF * P : (half + 1) * HALF * P, :]
+            nc.sync.dma_start(
+                out=tile_of[h][:, half * HALF : (half + 1) * HALF, :],
+                in_=rows.rearrange("(j p) d -> p j d", p=P),
+            )
+
+        def load(h):
+            q_raw[h] = raw.tile([P, TILES, D], BF16, name="q_raw")
+            k_raw[h] = raw.tile([P, TILES, D], BF16, name="k_raw")
+            v_raw[h] = raw.tile([P, TILES, D], BF16, name="v_raw")
+            for half in range(2):
+                load_half(q_raw, q_rot, h, half)
+                load_half(k_raw, k_scaled, h, half)
+            for half in range(2):
+                load_half(v_raw, v, h, half)
+
+        def turn(raw_tile, turned_tile, half):
+            bank = psum_turn.tile([P, D_PARTS, HALF, P], BF16, name="turn_bank")
+            for part in range(D_PARTS):
+                for j in range(HALF):
+                    nc.tensor.transpose(
+                        bank[:, part, j, :],
+                        raw_tile[:, half * HALF + j, part * P : (part + 1) * P],
+                        identity[:],
+                    )
+            nc.scalar.copy(
+                out=turned_tile[:, :, half * HALF * P : (half + 1) * HALF * P],
+                in_=bank[:].rearrange("p a j n -> p a (j n)"),
+            )
+
+        def make_decay(h):
+            decay[h] = decays.tile([P, TILES, P], F32, name="decay")
+            nc.scalar.activation(
+                out=decay[h][:],
+                in_=distance[:],
+                func=mybir.ActivationFunctionType.Exp,
+                scale=log_decay(h),
+            )
+
+        def regroup_values(h, c):
+            if c == 0:
+                v_grouped[h] = values_in.tile([P, 2, D, PACK], BF16, name="v_grouped", align_bytes=64)
+            nc.scalar.copy(
+                out=v_grouped[h][:, c].rearrange("p (b i) t -> p b t i", i=4),
+                in_=v_raw[h][:, c * PACK : (c + 1) * PACK, :].rearrange("p t (b i) -> p b t i", i=4),
+            )
+
+        def quantise_values(h):
+            v_codes[h] = values_in.tile([P, 2, D], U32, name="v_codes", align_bytes=64)
+            v_scales[h] = values_in.tile([P, 2, D], U8, name="v_scales", align_bytes=64)
+            nc.vector.quantize_mx(
+                out=v_codes[h][:].rearrange("p c d -> p (c d)").bitcast(FP8X4),
+                scales=v_scales[h][:].rearrange("p c d -> p (c d)"),
+                in_=v_grouped[h][:].rearrange("p c d t -> p (c d t)"),
+            )
+
+        def scores(h, k, i):
+            j, c = PAIRS[k][i]
+            sums = psum_sim.tile([P, PACK, P], F32, name="sums")
+            sim[(h, k, i)] = sums
+            for t in range(live_slots(j, c)):
+                key_tile = PACK * c + t
+                for part in range(D_PARTS):
+                    nc.tensor.matmul(
+                        sums[:, t, :],
+                        lhsT=k_turned[h][:, part, key_tile * P : (key_tile + 1) * P],
+                        rhs=q_turned[h][:, part, j * P : (j + 1) * P],
+                        start=(part == 0),
+                        stop=(part == D_PARTS - 1),
+                    )
+
+        def apply_decay(h, k, i):
+            j, c = PAIRS[k][i]
+            slots = live_slots(j, c)
+            first = TILES - 1 - (j - PACK * c)
+            nc.vector.tensor_tensor(
+                out=grouped[k][:, i, :, 0:slots],
+                in0=sim[(h, k, i)][:, 0:slots, :].rearrange("p t n -> p n t"),
+                in1=decay[h][:, first : first + slots, :].rearrange("p u n -> p n u"),
+                op=mybir.AluOpType.mult,
+            )
+
+        def quantise(h, k):
+            codes[(h, k)] = packed.tile([P, 2, P], U32, name="codes", align_bytes=64)
+            scales[(h, k)] = packed.tile([P, 2, P], U8, name="scales", align_bytes=64)
+            nc.vector.quantize_mx(
+                out=codes[(h, k)][:].rearrange("p i n -> p (i n)").bitcast(FP8X4),
+                scales=scales[(h, k)][:].rearrange("p i n -> p (i n)"),
+                in_=grouped[k][:].rearrange("p i n t -> p (i n t)"),
+            )
+
+        def weigh_values(h, k):
+            for i, (j, c) in enumerate(PAIRS[k]):
+                last_pass = c == j // PACK
+                if j == 0:
+                    result[h] = results.tile([P, TILES, D], F32, name="result")
+                if j % 2 == 0 and c == 0:
+                    ret["now"] = psum_ret.tile([P, 2, D], F32, name="ret_bank")
+                nc.tensor.matmul_mx(
+                    out=ret["now"][:, j % 2, :],
+                    lhsT=codes[(h, k)][:, i, :].bitcast(FP8X4),
+                    lhsT_scale=scales[(h, k)][:, i, :],
+                    rhs=v_codes[h][:, c, :].bitcast(FP8X4),
+                    rhs_scale=v_scales[h][:, c, :],
+                    start=(c == 0),
+                    stop=last_pass,
+                )
+                if j % 2 == 1 and last_pass:
+                    nc.scalar.copy(out=result[h][:, j - 1 : j + 1, :], in_=ret["now"][:])
+                if j % HALF == HALF - 1 and last_pass:
+                    nc.sync.dma_start(
+                        out=out_tiles[:, j + 1 - HALF : j + 1, h * D : (h + 1) * D],
+                        in_=result[h][:, j + 1 - HALF : j + 1, :],
+                    )
+
+        def start_head(h):
+            q_turned[h] = turned.tile([P, D_PARTS, N], BF16, name="q_turned")
+            k_turned[h] = turned.tile([P, D_PARTS, N], BF16, name="k_turned")
+
+        load(0)
+        load(1)
+        make_decay(0)
+        start_head(0)
+        turn(q_raw[0], q_turned[0], 0)
+        turn(k_raw[0], k_turned[0], 0)
+        regroup_values(0, 0)
+        regroup_values(0, 1)
+
+        steps = [(h, k) for h in range(H) for k in range(len(PAIRS))]
+        for g in range(len(steps) + MX_LAG):
+            if g < len(steps):
+                h, k = steps[g]
+                more = h + 1 < H
+                if k == 0 and h + 2 < H:
+                    load(h + 2)
+                scores(h, k, 0)
+                if k == 0:
+                    turn(q_raw[h], q_turned[h], 1)
+                if k == 1:
+                    turn(k_raw[h], k_turned[h], 1)
+                if k == 2 and more:
+                    start_head(h + 1)
+                    turn(q_raw[h + 1], q_turned[h + 1], 0)
+                if k == 3 and more:
+                    turn(k_raw[h + 1], k_turned[h + 1], 0)
+                scores(h, k, 1)
+                apply_decay(h, k, 0)
+            if 1 <= g <= len(steps):
+                quantise(*steps[g - 1])
+            if g < len(steps):
+                apply_decay(h, k, 1)
+                if k == 0:
+                    quantise_values(h)
+            if g >= MX_LAG:
+                weigh_values(*steps[g - MX_LAG])
+            if g < len(steps) and more:
+                if k == 0:
+                    make_decay(h + 1)
+                if k == 4:
+                    regroup_values(h + 1, 0)
+                if k == 5:
+                    regroup_values(h + 1, 1)

@@ -56,21 +56,21 @@ def tile_multiscaleretention_pb_kernel(tc, q_rot, k_scaled, v, out):
         identity = const.tile([P, P], BF16)
         make_identity(nc, identity[:])
 
-        distance = const.tile([P, TILES, P], F32)
+        distance = const.tile([P, P, TILES], F32)
         nc.gpsimd.iota(
             distance[:],
-            pattern=[[-P, TILES], [1, P]],
+            pattern=[[1, P], [-P, TILES]],
             base=P * (TILES - 1),
             channel_multiplier=-1,
             allow_small_or_imprecise_dtypes=True,
         )
         nc.gpsimd.affine_select(
-            out=distance[:, TILES - 1, :],
-            in_=distance[:, TILES - 1, :],
-            pattern=[[1, P]],
+            out=distance[:],
+            in_=distance[:],
+            pattern=[[1, P], [-P, TILES]],
             compare_op=mybir.AluOpType.is_ge,
             fill=FAR,
-            base=0,
+            base=P * (TILES - 1),
             channel_multiplier=-1,
         )
 
@@ -122,7 +122,7 @@ def tile_multiscaleretention_pb_kernel(tc, q_rot, k_scaled, v, out):
             )
 
         def make_decay(h):
-            decay[h] = decays.tile([P, TILES, P], F32, name="decay")
+            decay[h] = decays.tile([P, P, TILES], F32, name="decay")
             nc.scalar.activation(
                 out=decay[h][:],
                 in_=distance[:],
@@ -149,13 +149,13 @@ def tile_multiscaleretention_pb_kernel(tc, q_rot, k_scaled, v, out):
 
         def scores(h, k, i):
             j, c = PAIRS[k][i]
-            sums = psum_sim.tile([P, PACK, P], F32, name="sums")
+            sums = psum_sim.tile([P, P, PACK], F32, name="sums")
             sim[(h, k, i)] = sums
             for t in range(live_slots(j, c)):
                 key_tile = PACK * c + t
                 for part in range(D_PARTS):
                     nc.tensor.matmul(
-                        sums[:, t, :],
+                        sums[:, :, t],
                         lhsT=k_turned[h][:, part, key_tile * P : (key_tile + 1) * P],
                         rhs=q_turned[h][:, part, j * P : (j + 1) * P],
                         start=(part == 0),
@@ -168,8 +168,8 @@ def tile_multiscaleretention_pb_kernel(tc, q_rot, k_scaled, v, out):
             first = TILES - 1 - (j - PACK * c)
             nc.vector.tensor_tensor(
                 out=grouped[k][:, i, :, 0:slots],
-                in0=sim[(h, k, i)][:, 0:slots, :].rearrange("p t n -> p n t"),
-                in1=decay[h][:, first : first + slots, :].rearrange("p u n -> p n u"),
+                in0=sim[(h, k, i)][:, :, 0:slots],
+                in1=decay[h][:, :, first : first + slots],
                 op=mybir.AluOpType.mult,
             )
 
@@ -242,7 +242,7 @@ def tile_multiscaleretention_pb_kernel(tc, q_rot, k_scaled, v, out):
                 quantise(*steps[g - 1])
             if g < len(steps):
                 apply_decay(h, k, 1)
-                if k == 0:
+                if k == 1:
                     quantise_values(h)
             if g >= MX_LAG:
                 weigh_values(*steps[g - MX_LAG])

@@ -149,13 +149,13 @@ def tile_multiscaleretention_pb_kernel(tc, q_rot, k_scaled, v, out):
 
         def scores(h, k, i):
             j, c = PAIRS[k][i]
-            sums = psum_sim.tile([P, P, PACK], F32, name="sums")
+            sums = psum_sim.tile([P, PACK, P], F32, name="sums")
             sim[(h, k, i)] = sums
             for t in range(live_slots(j, c)):
                 key_tile = PACK * c + t
                 for part in range(D_PARTS):
                     nc.tensor.matmul(
-                        sums[:, :, t],
+                        sums[:, t, :],
                         lhsT=k_turned[h][:, part, key_tile * P : (key_tile + 1) * P],
                         rhs=q_turned[h][:, part, j * P : (j + 1) * P],
                         start=(part == 0),
@@ -168,7 +168,7 @@ def tile_multiscaleretention_pb_kernel(tc, q_rot, k_scaled, v, out):
             first = TILES - 1 - (j - PACK * c)
             nc.vector.tensor_tensor(
                 out=grouped[k][:, i, :, 0:slots],
-                in0=sim[(h, k, i)][:, :, 0:slots],
+                in0=sim[(h, k, i)][:, 0:slots, :].rearrange("p t n -> p n t"),
                 in1=decay[h][:, :, first : first + slots],
                 op=mybir.AluOpType.mult,
             )

@@ -17,12 +17,12 @@ P = 128
 PACK = 4
 TILES = N // P
 HALF = TILES // 2
-D_PARTS = D // P
+PAIR = 2
 
 BANKS = [(j, c) for j in range(TILES) for c in range(j // PACK + 1)]
 PAIRS = [(BANKS[b], BANKS[b + 1]) for b in range(0, len(BANKS), 2)]
 MX_LAG = 2
-FAR = 1.0e8
+FAR = 1.0e6
 
 FLOPS = 2 * 2 * H * D * len(BANKS) * P * PACK * P
 
@@ -53,7 +53,7 @@ def tile_multiscaleretention_pb_kernel(tc, q_rot, k_scaled, v, out):
         psum_ret = ctx.enter_context(tc.psum_pool(name="psum_ret", bufs=2))
         ctx.enter_context(tc.manual_schedule())
 
-        identity = const.tile([P, P], BF16)
+        identity = const.tile([P, P], F32)
         make_identity(nc, identity[:])
 
         distance = const.tile([P, P, TILES], F32)
@@ -64,14 +64,14 @@ def tile_multiscaleretention_pb_kernel(tc, q_rot, k_scaled, v, out):
             channel_multiplier=-1,
             allow_small_or_imprecise_dtypes=True,
         )
-        nc.gpsimd.affine_select(
-            out=distance[:],
-            in_=distance[:],
-            pattern=[[1, P], [-P, TILES]],
-            compare_op=mybir.AluOpType.is_ge,
-            fill=FAR,
-            base=P * (TILES - 1),
-            channel_multiplier=-1,
+        diagonal = distance[:, :, TILES - 1]
+        nc.vector.scalar_tensor_tensor(
+            out=diagonal,
+            in0=diagonal,
+            scalar=-FAR,
+            in1=diagonal,
+            op0=mybir.AluOpType.mult,
+            op1=mybir.AluOpType.max,
         )
 
         grouped = {}
@@ -108,17 +108,15 @@ def tile_multiscaleretention_pb_kernel(tc, q_rot, k_scaled, v, out):
                 load_half(v_raw, v, h, half)
 
         def turn(raw_tile, turned_tile, half):
-            bank = psum_turn.tile([P, D_PARTS, HALF, P], BF16, name="turn_bank")
-            for part in range(D_PARTS):
-                for j in range(HALF):
-                    nc.tensor.transpose(
-                        bank[:, part, j, :],
-                        raw_tile[:, half * HALF + j, part * P : (part + 1) * P],
-                        identity[:],
-                    )
+            bank = psum_turn.tile([P, HALF, P], F32, name="turn_bank")
+            for j in range(HALF):
+                nc.tensor.transpose(
+                    bank[:, j, :], raw_tile[:, half * HALF + j, :].bitcast(F32), identity[:]
+                )
+            words = turned_tile[:].rearrange("w n e -> w (n e)").bitcast(F32)
             nc.scalar.copy(
-                out=turned_tile[:, :, half * HALF * P : (half + 1) * HALF * P],
-                in_=bank[:].rearrange("p a j n -> p a (j n)"),
+                out=words[:, half * HALF * P : (half + 1) * HALF * P],
+                in_=bank[:].rearrange("w j n -> w (j n)"),
             )
 
         def make_decay(h):
@@ -153,13 +151,13 @@ def tile_multiscaleretention_pb_kernel(tc, q_rot, k_scaled, v, out):
             sim[(h, k, i)] = sums
             for t in range(live_slots(j, c)):
                 key_tile = PACK * c + t
-                for part in range(D_PARTS):
+                for e in range(PAIR):
                     nc.tensor.matmul(
                         sums[:, t, :],
-                        lhsT=k_turned[h][:, part, key_tile * P : (key_tile + 1) * P],
-                        rhs=q_turned[h][:, part, j * P : (j + 1) * P],
-                        start=(part == 0),
-                        stop=(part == D_PARTS - 1),
+                        lhsT=k_turned[h][:, key_tile * P : (key_tile + 1) * P, e],
+                        rhs=q_turned[h][:, j * P : (j + 1) * P, e],
+                        start=(e == 0),
+                        stop=(e == PAIR - 1),
                     )
 
         def apply_decay(h, k, i):
@@ -207,15 +205,15 @@ def tile_multiscaleretention_pb_kernel(tc, q_rot, k_scaled, v, out):
                     )
 
         def start_head(h):
-            q_turned[h] = turned.tile([P, D_PARTS, N], BF16, name="q_turned")
-            k_turned[h] = turned.tile([P, D_PARTS, N], BF16, name="k_turned")
+            q_turned[h] = turned.tile([P, N, PAIR], BF16, name="q_turned")
+            k_turned[h] = turned.tile([P, N, PAIR], BF16, name="k_turned")
 
         load(0)
         load(1)
-        make_decay(0)
         start_head(0)
         turn(q_raw[0], q_turned[0], 0)
         turn(k_raw[0], k_turned[0], 0)
+        make_decay(0)
         regroup_values(0, 0)
         regroup_values(0, 1)
 

@@ -15,13 +15,18 @@ N = 1024
 D = 256
 P = 128
 PACK = 4
-TILES = N // P
-HALF = TILES // 2
 PAIR = 2
+TILES = N // P
+PASSES = TILES // PACK
+QUARTERS = TILES // 2
 
 BANKS = [(j, c) for j in range(TILES) for c in range(j // PACK + 1)]
 PAIRS = [(BANKS[b], BANKS[b + 1]) for b in range(0, len(BANKS), 2)]
+STEPS = len(PAIRS)
 MX_LAG = 2
+AHEAD = 2
+QUARTER_DUE = [min(k for k in range(STEPS) if PAIRS[k][1][0] >= 2 * r) for r in range(QUARTERS)]
+PASS_DUE = [min(k for k in range(STEPS) if PAIRS[k][1][1] == c) for c in range(PASSES)]
 FAR = 1.0e6
 
 FLOPS = 2 * 2 * H * D * len(BANKS) * P * PACK * P
@@ -43,26 +48,34 @@ def tile_multiscaleretention_pb_kernel(tc, q_rot, k_scaled, v, out):
     with ExitStack() as ctx:
         const = ctx.enter_context(tc.tile_pool(name="const", bufs=1))
         raw = ctx.enter_context(tc.tile_pool(name="raw", bufs=3))
-        turned = ctx.enter_context(tc.tile_pool(name="turned", bufs=2))
-        decays = ctx.enter_context(tc.tile_pool(name="decays", bufs=3))
-        values_in = ctx.enter_context(tc.tile_pool(name="values_in", bufs=2))
+        turned_pool = ctx.enter_context(tc.tile_pool(name="turned_pool", bufs=2))
+        decays = ctx.enter_context(tc.tile_pool(name="decays", bufs=2))
+        values_in = ctx.enter_context(tc.tile_pool(name="values_in", bufs=2 * PASSES))
         packed = ctx.enter_context(tc.tile_pool(name="packed", bufs=4))
-        results = ctx.enter_context(tc.tile_pool(name="results", bufs=3))
+        results = ctx.enter_context(tc.tile_pool(name="results", bufs=4))
         psum_turn = ctx.enter_context(tc.psum_pool(name="psum_turn", bufs=2))
         psum_sim = ctx.enter_context(tc.psum_pool(name="psum_sim", bufs=4))
         psum_ret = ctx.enter_context(tc.psum_pool(name="psum_ret", bufs=2))
         ctx.enter_context(tc.manual_schedule())
 
+        within_tile = const.tile([P, P], F32)
+        nc.gpsimd.iota(
+            within_tile[:], pattern=[[1, P]], base=0, channel_multiplier=-1,
+            allow_small_or_imprecise_dtypes=True,
+        )
+        between_tiles = const.tile([P, TILES], F32)
+        nc.gpsimd.iota(
+            between_tiles[:], pattern=[[-P, TILES]], base=P * (TILES - 1), channel_multiplier=0,
+            allow_small_or_imprecise_dtypes=True,
+        )
         identity = const.tile([P, P], F32)
         make_identity(nc, identity[:])
-
         distance = const.tile([P, P, TILES], F32)
-        nc.gpsimd.iota(
-            distance[:],
-            pattern=[[1, P], [-P, TILES]],
-            base=P * (TILES - 1),
-            channel_multiplier=-1,
-            allow_small_or_imprecise_dtypes=True,
+        nc.vector.tensor_tensor(
+            out=distance[:],
+            in0=within_tile[:].unsqueeze(2).to_broadcast([P, P, TILES]),
+            in1=between_tiles[:].unsqueeze(1).to_broadcast([P, P, TILES]),
+            op=mybir.AluOpType.add,
         )
         diagonal = distance[:, :, TILES - 1]
         nc.vector.scalar_tensor_tensor(
@@ -81,42 +94,46 @@ def tile_multiscaleretention_pb_kernel(tc, q_rot, k_scaled, v, out):
                 if live_slots(j, c) < PACK:
                     nc.vector.memset(grouped[k][:, i], 0.0)
 
-        q_raw, k_raw, v_raw = {}, {}, {}
-        q_turned, k_turned = {}, {}
+        q_raw, k_raw = {}, {}
+        v_raw = {}
+        turned = {}
         decay = {}
         v_grouped, v_codes, v_scales = {}, {}, {}
         sim = {}
         codes, scales = {}, {}
         ret = {}
-        result = {}
-
-        def load_half(tile_of, source, h, half):
-            rows = source[0, h, half * HALF * P : (half + 1) * HALF * P, :]
-            nc.sync.dma_start(
-                out=tile_of[h][:, half * HALF : (half + 1) * HALF, :],
-                in_=rows.rearrange("(j p) d -> p j d", p=P),
-            )
 
         def load(h):
-            q_raw[h] = raw.tile([P, TILES, D], BF16, name="q_raw")
-            k_raw[h] = raw.tile([P, TILES, D], BF16, name="k_raw")
+            q_raw[h] = raw.tile([P, QUARTERS, 2, D], BF16, name="q_raw")
+            k_raw[h] = raw.tile([P, QUARTERS, 2, D], BF16, name="k_raw")
             v_raw[h] = raw.tile([P, TILES, D], BF16, name="v_raw")
-            for half in range(2):
-                load_half(q_raw, q_rot, h, half)
-                load_half(k_raw, k_scaled, h, half)
-            for half in range(2):
-                load_half(v_raw, v, h, half)
+            for r in range(QUARTERS):
+                for tile_of, source in ((q_raw, q_rot), (k_raw, k_scaled)):
+                    rows = source[0, h, r * 2 * P : (r + 1) * 2 * P, :]
+                    nc.sync.dma_start(
+                        out=tile_of[h][:, r], in_=rows.rearrange("(p r) d -> p r d", r=2)
+                    )
+                if r >= QUARTERS - PASSES:
+                    c = r - (QUARTERS - PASSES)
+                    rows = v[0, h, c * PACK * P : (c + 1) * PACK * P, :]
+                    nc.sync.dma_start(
+                        out=v_raw[h][:, c * PACK : (c + 1) * PACK, :],
+                        in_=rows.rearrange("(t p) d -> p t d", p=P),
+                    )
 
-        def turn(raw_tile, turned_tile, half):
-            bank = psum_turn.tile([P, HALF, P], F32, name="turn_bank")
-            for j in range(HALF):
-                nc.tensor.transpose(
-                    bank[:, j, :], raw_tile[:, half * HALF + j, :].bitcast(F32), identity[:]
-                )
-            words = turned_tile[:].rearrange("w n e -> w (n e)").bitcast(F32)
+        def turn(h, quarter):
+            if quarter == 0:
+                turned[h] = turned_pool.tile([P, QUARTERS, 2, 2 * P, PAIR], BF16, name="turned")
+            bank = psum_turn.tile([P, 2, 2, P], F32, name="turn_bank")
+            for a, raw_tile in enumerate((q_raw[h], k_raw[h])):
+                for r in range(2):
+                    nc.tensor.transpose(
+                        bank[:, a, r, :], raw_tile[:, quarter, r, :].bitcast(F32), identity[:]
+                    )
+            words = turned[h][:, quarter].rearrange("w a n e -> w (a n e)").bitcast(F32)
             nc.scalar.copy(
-                out=words[:, half * HALF * P : (half + 1) * HALF * P],
-                in_=bank[:].rearrange("w j n -> w (j n)"),
+                out=words.rearrange("w (a p r) -> w a p r", a=2, r=2),
+                in_=bank[:].rearrange("w a r p -> w a p r"),
             )
 
         def make_decay(h):
@@ -129,20 +146,19 @@ def tile_multiscaleretention_pb_kernel(tc, q_rot, k_scaled, v, out):
             )
 
         def regroup_values(h, c):
-            if c == 0:
-                v_grouped[h] = values_in.tile([P, 2, D, PACK], BF16, name="v_grouped", align_bytes=64)
+            v_grouped[(h, c)] = values_in.tile([P, D, PACK], BF16, name="v_grouped", align_bytes=64)
             nc.scalar.copy(
-                out=v_grouped[h][:, c].rearrange("p (b i) t -> p b t i", i=4),
+                out=v_grouped[(h, c)][:].rearrange("p (b i) t -> p b t i", i=4),
                 in_=v_raw[h][:, c * PACK : (c + 1) * PACK, :].rearrange("p t (b i) -> p b t i", i=4),
             )
 
-        def quantise_values(h):
-            v_codes[h] = values_in.tile([P, 2, D], U32, name="v_codes", align_bytes=64)
-            v_scales[h] = values_in.tile([P, 2, D], U8, name="v_scales", align_bytes=64)
+        def quantise_values(h, c):
+            v_codes[(h, c)] = values_in.tile([P, D], U32, name="v_codes", align_bytes=64)
+            v_scales[(h, c)] = values_in.tile([P, D], U8, name="v_scales", align_bytes=64)
             nc.vector.quantize_mx(
-                out=v_codes[h][:].rearrange("p c d -> p (c d)").bitcast(FP8X4),
-                scales=v_scales[h][:].rearrange("p c d -> p (c d)"),
-                in_=v_grouped[h][:].rearrange("p c d t -> p (c d t)"),
+                out=v_codes[(h, c)][:].bitcast(FP8X4),
+                scales=v_scales[(h, c)][:],
+                in_=v_grouped[(h, c)][:].rearrange("p d t -> p (d t)"),
             )
 
         def scores(h, k, i):
@@ -154,8 +170,8 @@ def tile_multiscaleretention_pb_kernel(tc, q_rot, k_scaled, v, out):
                 for e in range(PAIR):
                     nc.tensor.matmul(
                         sums[:, t, :],
-                        lhsT=k_turned[h][:, key_tile * P : (key_tile + 1) * P, e],
-                        rhs=q_turned[h][:, j * P : (j + 1) * P, e],
+                        lhsT=turned[h][:, key_tile // 2, 1, (key_tile % 2) * P : (key_tile % 2 + 1) * P, e],
+                        rhs=turned[h][:, j // 2, 0, (j % 2) * P : (j % 2 + 1) * P, e],
                         start=(e == 0),
                         stop=(e == PAIR - 1),
                     )
@@ -183,71 +199,56 @@ def tile_multiscaleretention_pb_kernel(tc, q_rot, k_scaled, v, out):
         def weigh_values(h, k):
             for i, (j, c) in enumerate(PAIRS[k]):
                 last_pass = c == j // PACK
-                if j == 0:
-                    result[h] = results.tile([P, TILES, D], F32, name="result")
                 if j % 2 == 0 and c == 0:
                     ret["now"] = psum_ret.tile([P, 2, D], F32, name="ret_bank")
                 nc.tensor.matmul_mx(
                     out=ret["now"][:, j % 2, :],
                     lhsT=codes[(h, k)][:, i, :].bitcast(FP8X4),
                     lhsT_scale=scales[(h, k)][:, i, :],
-                    rhs=v_codes[h][:, c, :].bitcast(FP8X4),
-                    rhs_scale=v_scales[h][:, c, :],
+                    rhs=v_codes[(h, c)][:].bitcast(FP8X4),
+                    rhs_scale=v_scales[(h, c)][:],
                     start=(c == 0),
                     stop=last_pass,
                 )
                 if j % 2 == 1 and last_pass:
-                    nc.scalar.copy(out=result[h][:, j - 1 : j + 1, :], in_=ret["now"][:])
-                if j % HALF == HALF - 1 and last_pass:
+                    result = results.tile([P, 2, D], F32, name="result")
+                    nc.scalar.copy(out=result[:], in_=ret["now"][:])
                     nc.sync.dma_start(
-                        out=out_tiles[:, j + 1 - HALF : j + 1, h * D : (h + 1) * D],
-                        in_=result[h][:, j + 1 - HALF : j + 1, :],
+                        out=out_tiles[:, j - 1 : j + 1, h * D : (h + 1) * D], in_=result[:]
                     )
-
-        def start_head(h):
-            q_turned[h] = turned.tile([P, N, PAIR], BF16, name="q_turned")
-            k_turned[h] = turned.tile([P, N, PAIR], BF16, name="k_turned")
 
         load(0)
         load(1)
-        start_head(0)
-        turn(q_raw[0], q_turned[0], 0)
-        turn(k_raw[0], k_turned[0], 0)
-        make_decay(0)
-        regroup_values(0, 0)
-        regroup_values(0, 1)
-
-        steps = [(h, k) for h in range(H) for k in range(len(PAIRS))]
-        for g in range(len(steps) + MX_LAG):
-            if g < len(steps):
-                h, k = steps[g]
-                more = h + 1 < H
-                if k == 0 and h + 2 < H:
-                    load(h + 2)
+        last_step = H * STEPS - 1
+        for g in range(-AHEAD, last_step + 1 + MX_LAG):
+            h, k = divmod(g, STEPS)
+            computing = 0 <= g <= last_step
+            near = [(head, g - head * STEPS) for head in (h, h + 1) if 0 <= head < H]
+            if computing and k == 0 and h + 2 < H:
+                load(h + 2)
+            for head, step in near:
+                if step == -AHEAD:
+                    make_decay(head)
+            if computing:
                 scores(h, k, 0)
-                if k == 0:
-                    turn(q_raw[h], q_turned[h], 1)
-                if k == 1:
-                    turn(k_raw[h], k_turned[h], 1)
-                if k == 2 and more:
-                    start_head(h + 1)
-                    turn(q_raw[h + 1], q_turned[h + 1], 0)
-                if k == 3 and more:
-                    turn(k_raw[h + 1], k_turned[h + 1], 0)
+            for head, step in near:
+                for quarter in range(QUARTERS):
+                    if step == QUARTER_DUE[quarter] - AHEAD:
+                        turn(head, quarter)
+            if computing:
                 scores(h, k, 1)
                 apply_decay(h, k, 0)
-            if 1 <= g <= len(steps):
-                quantise(*steps[g - 1])
-            if g < len(steps):
+            if 0 <= g - 1 <= last_step:
+                quantise(*divmod(g - 1, STEPS))
+            if computing:
                 apply_decay(h, k, 1)
-                if k == 1:
-                    quantise_values(h)
-            if g >= MX_LAG:
-                weigh_values(*steps[g - MX_LAG])
-            if g < len(steps) and more:
-                if k == 0:
-                    make_decay(h + 1)
-                if k == 4:
-                    regroup_values(h + 1, 0)
-                if k == 5:
-                    regroup_values(h + 1, 1)
+            for head, step in near:
+                for c in range(PASSES):
+                    if step == PASS_DUE[c] + MX_LAG - 1:
+                        quantise_values(head, c)
+            if 0 <= g - MX_LAG:
+                weigh_values(*divmod(g - MX_LAG, STEPS))
+            for head, step in near:
+                for c in range(PASSES):
+                    if step == PASS_DUE[c] + MX_LAG - 2:
+                        regroup_values(head, c)

@@ -51,6 +51,7 @@ def tile_multiscaleretention_pb_kernel(tc, q_rot, k_scaled, v, out):
         turned_pool = ctx.enter_context(tc.tile_pool(name="turned_pool", bufs=2))
         decays = ctx.enter_context(tc.tile_pool(name="decays", bufs=2))
         values_in = ctx.enter_context(tc.tile_pool(name="values_in", bufs=2 * PASSES))
+        staging = ctx.enter_context(tc.tile_pool(name="staging", bufs=2))
         packed = ctx.enter_context(tc.tile_pool(name="packed", bufs=4))
         results = ctx.enter_context(tc.tile_pool(name="results", bufs=4))
         psum_turn = ctx.enter_context(tc.psum_pool(name="psum_turn", bufs=2))
@@ -180,12 +181,22 @@ def tile_multiscaleretention_pb_kernel(tc, q_rot, k_scaled, v, out):
             j, c = PAIRS[k][i]
             slots = live_slots(j, c)
             first = TILES - 1 - (j - PACK * c)
-            nc.vector.tensor_tensor(
-                out=grouped[k][:, i, :, 0:slots],
-                in0=sim[(h, k, i)][:, 0:slots, :].rearrange("p t n -> p n t"),
-                in1=decay[h][:, :, first : first + slots],
-                op=mybir.AluOpType.mult,
-            )
+            if slots == 1:
+                staged = staging.tile([P, P], F32, name="staged")
+                nc.scalar.copy(out=staged[:], in_=sim[(h, k, i)][:, 0, :])
+                nc.gpsimd.tensor_tensor(
+                    out=grouped[k][:, i, :, 0],
+                    in0=staged[:],
+                    in1=decay[h][:, :, first],
+                    op=mybir.AluOpType.mult,
+                )
+            else:
+                nc.vector.tensor_tensor(
+                    out=grouped[k][:, i, :, 0:slots],
+                    in0=sim[(h, k, i)][:, 0:slots, :].rearrange("p t n -> p n t"),
+                    in1=decay[h][:, :, first : first + slots],
+                    op=mybir.AluOpType.mult,
+                )
 
         def quantise(h, k):
             codes[(h, k)] = packed.tile([P, 2, P], U32, name="codes", align_bytes=64)

@@ -51,7 +51,6 @@ def tile_multiscaleretention_pb_kernel(tc, q_rot, k_scaled, v, out):
         turned_pool = ctx.enter_context(tc.tile_pool(name="turned_pool", bufs=2))
         decays = ctx.enter_context(tc.tile_pool(name="decays", bufs=2))
         values_in = ctx.enter_context(tc.tile_pool(name="values_in", bufs=2 * PASSES))
-        staging = ctx.enter_context(tc.tile_pool(name="staging", bufs=2))
         packed = ctx.enter_context(tc.tile_pool(name="packed", bufs=4))
         results = ctx.enter_context(tc.tile_pool(name="results", bufs=4))
         psum_turn = ctx.enter_context(tc.psum_pool(name="psum_turn", bufs=2))
@@ -148,9 +147,13 @@ def tile_multiscaleretention_pb_kernel(tc, q_rot, k_scaled, v, out):
 
         def regroup_values(h, c):
             v_grouped[(h, c)] = values_in.tile([P, D, PACK], BF16, name="v_grouped", align_bytes=64)
-            nc.scalar.copy(
-                out=v_grouped[(h, c)][:].rearrange("p (b i) t -> p b t i", i=4),
-                in_=v_raw[h][:, c * PACK : (c + 1) * PACK, :].rearrange("p t (b i) -> p b t i", i=4),
+            nc.gpsimd.tensor_scalar(
+                out=v_grouped[(h, c)][:],
+                in0=v_raw[h][:, c * PACK : (c + 1) * PACK, :].rearrange("p t d -> p d t"),
+                scalar1=1.0,
+                scalar2=0.0,
+                op0=mybir.AluOpType.mult,
+                op1=mybir.AluOpType.add,
             )
 
         def quantise_values(h, c):
@@ -181,22 +184,12 @@ def tile_multiscaleretention_pb_kernel(tc, q_rot, k_scaled, v, out):
             j, c = PAIRS[k][i]
             slots = live_slots(j, c)
             first = TILES - 1 - (j - PACK * c)
-            if slots == 1:
-                staged = staging.tile([P, P], F32, name="staged")
-                nc.scalar.copy(out=staged[:], in_=sim[(h, k, i)][:, 0, :])
-                nc.gpsimd.tensor_tensor(
-                    out=grouped[k][:, i, :, 0],
-                    in0=staged[:],
-                    in1=decay[h][:, :, first],
-                    op=mybir.AluOpType.mult,
-                )
-            else:
-                nc.vector.tensor_tensor(
-                    out=grouped[k][:, i, :, 0:slots],
-                    in0=sim[(h, k, i)][:, 0:slots, :].rearrange("p t n -> p n t"),
-                    in1=decay[h][:, :, first : first + slots],
-                    op=mybir.AluOpType.mult,
-                )
+            nc.vector.tensor_tensor(
+                out=grouped[k][:, i, :, 0:slots],
+                in0=sim[(h, k, i)][:, 0:slots, :].rearrange("p t n -> p n t"),
+                in1=decay[h][:, :, first : first + slots],
+                op=mybir.AluOpType.mult,
+            )
 
         def quantise(h, k):
             codes[(h, k)] = packed.tile([P, 2, P], U32, name="codes", align_bytes=64)

import math
from contextlib import ExitStack

import concourse.mybir as mybir
from concourse.masks import make_identity

BF16 = mybir.dt.bfloat16
F32 = mybir.dt.float32
U32 = mybir.dt.uint32
U8 = mybir.dt.uint8
FP8X4 = mybir.dt.float8_e4m3fn_x4

H = 8
N = 1024
D = 256
P = 128
PACK = 4
PAIR = 2
TILES = N // P
PASSES = TILES // PACK
QUARTERS = TILES // 2

BANKS = [(j, c) for j in range(TILES) for c in range(j // PACK + 1)]
PAIRS = [(BANKS[b], BANKS[b + 1]) for b in range(0, len(BANKS), 2)]
STEPS = len(PAIRS)
MX_LAG = 2
AHEAD = 2
QUARTER_DUE = [min(k for k in range(STEPS) if PAIRS[k][1][0] >= 2 * r) for r in range(QUARTERS)]
PASS_DUE = [min(k for k in range(STEPS) if PAIRS[k][1][1] == c) for c in range(PASSES)]
FAR = 1.0e6

FLOPS = 2 * 2 * H * D * len(BANKS) * P * PACK * P


def live_slots(j, c):
    return min(PACK, j - PACK * c + 1)


def log_decay(h):
    first, last = math.log(2.0 ** -5), math.log(2.0 ** -9)
    return math.log(1.0 - math.exp(first + (last - first) * h / (H - 1)))


def tile_multiscaleretention_pb_kernel(tc, q_rot, k_scaled, v, out):
    nc = tc.nc
    out_tiles = out[0].rearrange("(j p) e -> p j e", p=P)

    with ExitStack() as ctx:
        const = ctx.enter_context(tc.tile_pool(name="const", bufs=1))
        raw = ctx.enter_context(tc.tile_pool(name="raw", bufs=3))
        turned_pool = ctx.enter_context(tc.tile_pool(name="turned_pool", bufs=2))
        decays = ctx.enter_context(tc.tile_pool(name="decays", bufs=2))
        values_in = ctx.enter_context(tc.tile_pool(name="values_in", bufs=2 * PASSES))
        packed = ctx.enter_context(tc.tile_pool(name="packed", bufs=4))
        results = ctx.enter_context(tc.tile_pool(name="results", bufs=4))
        psum_turn = ctx.enter_context(tc.psum_pool(name="psum_turn", bufs=2))
        psum_sim = ctx.enter_context(tc.psum_pool(name="psum_sim", bufs=4))
        psum_ret = ctx.enter_context(tc.psum_pool(name="psum_ret", bufs=2))
        ctx.enter_context(tc.manual_schedule())

        within_tile = const.tile([P, P], F32)
        nc.gpsimd.iota(
            within_tile[:], pattern=[[1, P]], base=0, channel_multiplier=-1,
            allow_small_or_imprecise_dtypes=True,
        )
        between_tiles = const.tile([P, TILES], F32)
        nc.gpsimd.iota(
            between_tiles[:], pattern=[[-P, TILES]], base=P * (TILES - 1), channel_multiplier=0,
            allow_small_or_imprecise_dtypes=True,
        )
        identity = const.tile([P, P], F32)
        make_identity(nc, identity[:])
        distance = const.tile([P, P, TILES], F32)
        nc.vector.tensor_tensor(
            out=distance[:],
            in0=within_tile[:].unsqueeze(2).to_broadcast([P, P, TILES]),
            in1=between_tiles[:].unsqueeze(1).to_broadcast([P, P, TILES]),
            op=mybir.AluOpType.add,
        )
        diagonal = distance[:, :, TILES - 1]
        nc.vector.scalar_tensor_tensor(
            out=diagonal,
            in0=diagonal,
            scalar=-FAR,
            in1=diagonal,
            op0=mybir.AluOpType.mult,
            op1=mybir.AluOpType.max,
        )

        grouped = {}
        for k, pair in enumerate(PAIRS):
            grouped[k] = const.tile([P, 2, P, PACK], BF16, name="grouped%d" % k, align_bytes=64)
            for i, (j, c) in enumerate(pair):
                if live_slots(j, c) < PACK:
                    nc.vector.memset(grouped[k][:, i], 0.0)

        q_raw, k_raw = {}, {}
        v_raw = {}
        turned = {}
        decay = {}
        v_grouped, v_codes, v_scales = {}, {}, {}
        sim = {}
        codes, scales = {}, {}
        ret = {}

        def load(h):
            q_raw[h] = raw.tile([P, QUARTERS, 2, D], BF16, name="q_raw")
            k_raw[h] = raw.tile([P, QUARTERS, 2, D], BF16, name="k_raw")
            v_raw[h] = raw.tile([P, TILES, D], BF16, name="v_raw")
            for r in range(QUARTERS):
                for tile_of, source in ((q_raw, q_rot), (k_raw, k_scaled)):
                    rows = source[0, h, r * 2 * P : (r + 1) * 2 * P, :]
                    nc.sync.dma_start(
                        out=tile_of[h][:, r], in_=rows.rearrange("(p r) d -> p r d", r=2)
                    )
                if r >= QUARTERS - PASSES:
                    c = r - (QUARTERS - PASSES)
                    rows = v[0, h, c * PACK * P : (c + 1) * PACK * P, :]
                    nc.sync.dma_start(
                        out=v_raw[h][:, c * PACK : (c + 1) * PACK, :],
                        in_=rows.rearrange("(t p) d -> p t d", p=P),
                    )

        def turn(h, quarter):
            if quarter == 0:
                turned[h] = turned_pool.tile([P, QUARTERS, 2, 2 * P, PAIR], BF16, name="turned")
            bank = psum_turn.tile([P, 2, 2, P], F32, name="turn_bank")
            for a, raw_tile in enumerate((q_raw[h], k_raw[h])):
                for r in range(2):
                    nc.tensor.transpose(
                        bank[:, a, r, :], raw_tile[:, quarter, r, :].bitcast(F32), identity[:]
                    )
            words = turned[h][:, quarter].rearrange("w a n e -> w (a n e)").bitcast(F32)
            nc.scalar.copy(
                out=words.rearrange("w (a p r) -> w a p r", a=2, r=2),
                in_=bank[:].rearrange("w a r p -> w a p r"),
            )

        def make_decay(h):
            decay[h] = decays.tile([P, P, TILES], F32, name="decay")
            nc.scalar.activation(
                out=decay[h][:],
                in_=distance[:],
                func=mybir.ActivationFunctionType.Exp,
                scale=log_decay(h),
            )

        def regroup_values(h, c):
            v_grouped[(h, c)] = values_in.tile([P, D, PACK], BF16, name="v_grouped", align_bytes=64)
            nc.gpsimd.tensor_scalar(
                out=v_grouped[(h, c)][:],
                in0=v_raw[h][:, c * PACK : (c + 1) * PACK, :].rearrange("p t d -> p d t"),
                scalar1=1.0,
                scalar2=0.0,
                op0=mybir.AluOpType.mult,
                op1=mybir.AluOpType.add,
            )

        def quantise_values(h, c):
            v_codes[(h, c)] = values_in.tile([P, D], U32, name="v_codes", align_bytes=64)
            v_scales[(h, c)] = values_in.tile([P, D], U8, name="v_scales", align_bytes=64)
            nc.vector.quantize_mx(
                out=v_codes[(h, c)][:].bitcast(FP8X4),
                scales=v_scales[(h, c)][:],
                in_=v_grouped[(h, c)][:].rearrange("p d t -> p (d t)"),
            )

        def scores(h, k, i):
            j, c = PAIRS[k][i]
            sums = psum_sim.tile([P, PACK, P], F32, name="sums")
            sim[(h, k, i)] = sums
            for t in range(live_slots(j, c)):
                key_tile = PACK * c + t
                for e in range(PAIR):
                    nc.tensor.matmul(
                        sums[:, t, :],
                        lhsT=turned[h][:, key_tile // 2, 1, (key_tile % 2) * P : (key_tile % 2 + 1) * P, e],
                        rhs=turned[h][:, j // 2, 0, (j % 2) * P : (j % 2 + 1) * P, e],
                        start=(e == 0),
                        stop=(e == PAIR - 1),
                    )

        def apply_decay(h, k, i):
            j, c = PAIRS[k][i]
            slots = live_slots(j, c)
            first = TILES - 1 - (j - PACK * c)
            nc.vector.tensor_tensor(
                out=grouped[k][:, i, :, 0:slots],
                in0=sim[(h, k, i)][:, 0:slots, :].rearrange("p t n -> p n t"),
                in1=decay[h][:, :, first : first + slots],
                op=mybir.AluOpType.mult,
            )

        def quantise(h, k):
            codes[(h, k)] = packed.tile([P, 2, P], U32, name="codes", align_bytes=64)
            scales[(h, k)] = packed.tile([P, 2, P], U8, name="scales", align_bytes=64)
            nc.vector.quantize_mx(
                out=codes[(h, k)][:].rearrange("p i n -> p (i n)").bitcast(FP8X4),
                scales=scales[(h, k)][:].rearrange("p i n -> p (i n)"),
                in_=grouped[k][:].rearrange("p i n t -> p (i n t)"),
            )

        def weigh_values(h, k):
            for i, (j, c) in enumerate(PAIRS[k]):
                last_pass = c == j // PACK
                if j % 2 == 0 and c == 0:
                    ret["now"] = psum_ret.tile([P, 2, D], F32, name="ret_bank")
                nc.tensor.matmul_mx(
                    out=ret["now"][:, j % 2, :],
                    lhsT=codes[(h, k)][:, i, :].bitcast(FP8X4),
                    lhsT_scale=scales[(h, k)][:, i, :],
                    rhs=v_codes[(h, c)][:].bitcast(FP8X4),
                    rhs_scale=v_scales[(h, c)][:],
                    start=(c == 0),
                    stop=last_pass,
                )
                if j % 2 == 1 and last_pass:
                    result = results.tile([P, 2, D], F32, name="result")
                    nc.scalar.copy(out=result[:], in_=ret["now"][:])
                    nc.sync.dma_start(
                        out=out_tiles[:, j - 1 : j + 1, h * D : (h + 1) * D], in_=result[:]
                    )

        load(0)
        load(1)
        last_step = H * STEPS - 1
        for g in range(-AHEAD, last_step + 1 + MX_LAG):
            h, k = divmod(g, STEPS)
            computing = 0 <= g <= last_step
            near = [(head, g - head * STEPS) for head in (h, h + 1) if 0 <= head < H]
            if computing and k == 0 and h + 2 < H:
                load(h + 2)
            for head, step in near:
                if step == -AHEAD:
                    make_decay(head)
            if computing:
                scores(h, k, 0)
            for head, step in near:
                for quarter in range(QUARTERS):
                    if step == QUARTER_DUE[quarter] - AHEAD:
                        turn(head, quarter)
            if computing:
                scores(h, k, 1)
                apply_decay(h, k, 0)
            if 0 <= g - 1 <= last_step:
                quantise(*divmod(g - 1, STEPS))
            if computing:
                apply_decay(h, k, 1)
            for head, step in near:
                for c in range(PASSES):
                    if step == PASS_DUE[c] + MX_LAG - 1:
                        quantise_values(head, c)
            if 0 <= g - MX_LAG:
                weigh_values(*divmod(g - MX_LAG, STEPS))
            for head, step in near:
                for c in range(PASSES):
                    if step == PASS_DUE[c] + MX_LAG - 2:
                        regroup_values(head, c)
